import numpy as np
import ml_dtypes

BF16 = ml_dtypes.bfloat16


def bf(x):
    return np.asarray(x, np.float32).astype(BF16)


def f32(x):
    return np.asarray(x, np.float32)


def f64(x):
    return np.asarray(x).astype(np.float64)


def striped(idx):
    return np.tile(idx.reshape(-1, 16).T, (8, 1))


S, CF, HID, NH, B, T, DH, P, N = 3072, 128, 128, 128, 2, 128, 128, 64, 4096
F = T // P
SCALE = DH ** -0.5
TERMS = 150


def erf(a):
    c = np.clip(a, -6.0, 6.0)
    term = c.copy()
    total = c.copy()
    for n in range(TERMS):
        term = term * (2.0 * c * c) / (2.0 * n + 3.0)
        total = total + term
    r = 2.0 / np.sqrt(np.pi) * np.exp(-c * c) * total
    return np.where(np.abs(a) > 6.0, np.sign(a), r)


def gelu_erf(x):
    return 0.5 * x * (1.0 + erf(x / np.sqrt(2.0)))


def setup_inputs():
    return {
        "rel_table": bf(np.random.uniform(-1.0, 1.0, (S, CF))),
        "w1": bf(np.random.standard_normal((CF, HID)) * np.sqrt(3.0 / CF)),
        "b1": f32(0.1 * np.random.standard_normal((HID, 1))),
        "w2": bf(1.5 * np.random.standard_normal((HID, NH)) / np.sqrt(HID)),
        "q": bf(np.random.standard_normal((NH, B, DH, T))),
        "k": bf(np.random.standard_normal((NH, B, DH, T))),
        "v": bf(np.random.standard_normal((NH, B, T, DH))),
        "offs": striped(np.random.permutation(np.tile(np.arange(S), 2))[:N]),
    }


def reference(rel_table, w1, b1, w2, q, k, v, offs):
    idx = offs[:16].T.reshape(-1)
    hid = gelu_erf(f64(rel_table) @ f64(w1) + f64(b1).T)
    bias = f64(w2).T @ hid[idx].T
    bias = np.tile(bias.reshape(NH, P, P), (1, F, F))
    s = SCALE * np.matmul(f64(q).transpose(0, 1, 3, 2), f64(k)) + bias[:, None]
    e = np.exp(s - s.max(axis=-1, keepdims=True))
    p = e / e.sum(axis=-1, keepdims=True)
    return np.matmul(p, f64(v))

@@ -1,0 +1,204 @@
+import concourse.mybir as mybir
+from concourse.masks import make_identity
+
+BF16 = mybir.dt.bfloat16
+F32 = mybir.dt.float32
+I32 = mybir.dt.int32
+U16 = mybir.dt.uint16
+ACT = mybir.ActivationFunctionType
+ALU = mybir.AluOpType
+
+P = 128
+ROWS, CF, HID, NH, B, T, DH, PLACES, N = 3072, 128, 128, 128, 2, 128, 128, 64, 4096
+SCALE = DH**-0.5
+FLOPS = 2 * ROWS * CF * HID + 2 * N * HID * NH + 2 * 2 * NH * B * T * T * DH
+
+BANK = 512
+PIECE = 512
+HALF = 32
+
+HEADS_PER_LOAD = 8
+TILES_PER_LOAD = HEADS_PER_LOAD * B
+N_LOADS = NH // HEADS_PER_LOAD
+PREFETCH = 10
+HEADS_PER_BANK = 2
+TILES_PER_BANK = HEADS_PER_BANK * B
+BANKS_PER_LOAD = TILES_PER_LOAD // TILES_PER_BANK
+
+
+def tile_flexattentioncpb_b_kernel(tc, rel_table, w1, b1, w2, q, k, v, offs, out):
+    nc = tc.nc
+    with (
+        tc.tile_pool(name="held", bufs=1) as held,
+        tc.tile_pool(name="inputs", bufs=PREFETCH) as inputs,
+    ):
+        offsets = held.tile([P, N // 16], U16, name="offsets")
+        nc.sync.dma_start(offsets[:], offs)
+        w1_t = held.tile([CF, HID], BF16, name="w1_t")
+        nc.scalar.dma_start(w1_t[:], w1)
+        w2_t = held.tile([HID, NH], BF16, name="w2_t")
+        nc.scalar.dma_start(w2_t[:], w2)
+        b1_t = held.tile([HID, 1], F32, name="b1_t")
+        nc.scalar.dma_start(b1_t[:], b1)
+
+        def load_group(g):
+            heads = slice(g * HEADS_PER_LOAD, (g + 1) * HEADS_PER_LOAD)
+            q_t = inputs.tile([DH, TILES_PER_LOAD, T], BF16, name="q_t")
+            k_t = inputs.tile([DH, TILES_PER_LOAD, T], BF16, name="k_t")
+            v_t = inputs.tile([T, TILES_PER_LOAD, DH], BF16, name="v_t")
+            nc.sync.dma_start(q_t[:], q[heads].rearrange("h n d t -> d (h n) t"))
+            nc.sync.dma_start(k_t[:], k[heads].rearrange("h n d t -> d (h n) t"))
+            nc.sync.dma_start(v_t[:], v[heads].rearrange("h n u d -> u (h n) d"))
+            return q_t, k_t, v_t
+
+        ident = held.tile([P, P], BF16, name="ident")
+        make_identity(nc, ident[:])
+        diff = held.tile([P, 2, PLACES], I32, name="diff")
+        nc.gpsimd.iota(diff[:], pattern=[[0, 2], [2, PLACES]], base=0, channel_multiplier=-1)
+        pick = []
+        for a in range(2):
+            pick_a = held.tile([P, 2, PLACES], BF16, name="pick%d" % a)
+            nc.vector.tensor_scalar(pick_a[:], diff[:], float(-a), None, op0=ALU.is_equal)
+            pick.append(pick_a)
+
+        hid_t = held.tile([HID, ROWS], BF16, name="hid_t")
+        bias_x = held.tile([P, NH, HALF], BF16, name="bias_x")
+
+        with (
+            tc.tile_pool(name="setup", bufs=1) as setup,
+            tc.psum_pool(name="setup_psum", bufs=2) as setup_psum,
+        ):
+            rel_flip = setup.tile([CF, ROWS], BF16, name="rel_flip")
+            rel_parts = []
+            for c in range(3):
+                rel_c = setup.tile([P, 8, CF], BF16, name="rel%d" % c)
+                nc.sync.dma_start(
+                    rel_c[:], rel_table[c * 1024 : (c + 1) * 1024, :].rearrange("(a p) c -> p a c", p=P)
+                )
+                rel_parts.append(rel_c)
+
+            loaded = [load_group(g) for g in range(PREFETCH)]
+
+            for c in range(3):
+                flipped = setup_psum.tile([P, 8, P], BF16, name="flipped")
+                for a in range(8):
+                    nc.tensor.transpose(flipped[:, a, :], rel_parts[c][:, a, :], ident[:])
+                nc.vector.tensor_copy(
+                    rel_flip[:, c * 1024 : (c + 1) * 1024], flipped[:].rearrange("c a p -> c (a p)")
+                )
+            for blk in range(ROWS // BANK):
+                cols = slice(blk * BANK, (blk + 1) * BANK)
+                hid_ps = setup_psum.tile([P, BANK], F32, name="hid_ps", tag="product", bufs=4)
+                nc.tensor.matmul(hid_ps[:], w1_t[:], rel_flip[:, cols], start=True, stop=True)
+                nc.scalar.activation(hid_t[:, cols], hid_ps[:], ACT.Gelu, bias=b1_t[:, 0:1])
+
+            bias_h = setup.tile([NH, P, HALF], BF16, name="bias_h")
+            bias_flat = bias_h[:].rearrange("h m c -> h (m c)")
+            for piece in range(N // PIECE):
+                bias_ps = setup_psum.tile([P, PIECE], F32, name="bias_ps", tag="product", bufs=4)
+                nc.tensor.matmul(
+                    bias_ps[:],
+                    w2_t[:],
+                    hid_t[:].indirect(offsets[:, piece * (PIECE // 16) : (piece + 1) * (PIECE // 16)]),
+                    start=True,
+                    stop=True,
+                )
+                cols = slice(piece * PIECE, (piece + 1) * PIECE)
+                if piece % 2 == 0:
+                    nc.scalar.mul(bias_flat[:, cols], bias_ps[:], 1.0 / SCALE)
+                else:
+                    nc.vector.tensor_scalar(bias_flat[:, cols], bias_ps[:], 1.0 / SCALE, None, op0=ALU.mult)
+
+            for blk in range(HALF // 8):
+                flipped = setup_psum.tile([P, 8, P], BF16, name="flipped")
+                for c in range(8):
+                    nc.tensor.transpose(flipped[:, c, :], bias_h[:, :, blk * 8 + c], ident[:])
+                by_head = flipped[:].rearrange("m c h -> m h c")
+                if blk % 2 == 0:
+                    nc.vector.tensor_copy(bias_x[:, :, blk * 8 : (blk + 1) * 8], by_head)
+                else:
+                    nc.scalar.copy(bias_x[:, :, blk * 8 : (blk + 1) * 8], by_head)
+
+        with (
+            tc.tile_pool(name="work", bufs=3) as work,
+            tc.tile_pool(name="stats", bufs=4) as stats,
+            tc.tile_pool(name="staging", bufs=2) as staging,
+            tc.psum_pool(name="score_psum", bufs=3) as score_psum,
+            tc.psum_pool(name="flip_psum", bufs=2) as flip_psum,
+            tc.psum_pool(name="out_psum", bufs=3) as out_psum,
+        ):
+            for g in range(N_LOADS):
+                q_t, k_t, v_t = loaded[g]
+                staged = staging.tile([T, TILES_PER_LOAD, DH], F32, name="staged")
+                for bank in range(BANKS_PER_LOAD):
+                    first = bank * TILES_PER_BANK
+                    head = g * HEADS_PER_LOAD + bank * HEADS_PER_BANK
+
+                    scores = score_psum.tile([T, BANK], F32, name="scores")
+                    by_half = scores[:].rearrange(
+                        "t (h r a c) -> t h r a c", h=HEADS_PER_BANK, r=2 * B, a=2
+                    )
+                    for a in range(2):
+                        nc.tensor.matmul(
+                            by_half[:, :, :, a, :],
+                            pick[a][:].rearrange("m f t -> m (f t)"),
+                            bias_x[:, head : head + HEADS_PER_BANK, :]
+                            .unsqueeze(2)
+                            .to_broadcast([P, HEADS_PER_BANK, 2 * B, HALF]),
+                            start=(a == 0),
+                            stop=False,
+                        )
+                    for i in range(TILES_PER_BANK):
+                        nc.tensor.matmul(
+                            scores[:, i * T : (i + 1) * T],
+                            q_t[:, first + i, :],
+                            k_t[:, first + i, :],
+                            start=False,
+                            stop=(i == TILES_PER_BANK - 1),
+                        )
+
+                    row_max = stats.tile([T, TILES_PER_BANK], F32, name="row_max")
+                    nc.vector.tensor_reduce(
+                        row_max[:],
+                        scores[:].rearrange("t (i u) -> t i u", i=TILES_PER_BANK),
+                        axis=mybir.AxisListType.X,
+                        op=ALU.max,
+                    )
+                    shift = stats.tile([T, TILES_PER_BANK], F32, name="shift")
+                    nc.vector.tensor_scalar(shift[:], row_max[:], -SCALE, None, op0=ALU.mult)
+                    weights = work.tile([T, TILES_PER_BANK, T], BF16, name="weights")
+                    row_sum = stats.tile([T, TILES_PER_BANK], F32, name="row_sum")
+                    for i in range(TILES_PER_BANK):
+                        nc.scalar.activation(
+                            weights[:, i, :],
+                            scores[:, i * T : (i + 1) * T],
+                            ACT.Exp,
+                            bias=shift[:, i : i + 1],
+                            scale=SCALE,
+                            accum_out=row_sum[:, i : i + 1],
+                        )
+
+                    flip_ps = flip_psum.tile([T, TILES_PER_BANK, T], BF16, name="flip_ps")
+                    for i in range(TILES_PER_BANK):
+                        nc.tensor.transpose(flip_ps[:, i, :], weights[:, i, :], ident[:])
+                    weights_flip = work.tile([T, TILES_PER_BANK, T], BF16, name="weights_flip")
+                    nc.scalar.copy(weights_flip[:], flip_ps[:])
+
+                    out_ps = out_psum.tile([T, TILES_PER_BANK, DH], F32, name="out_ps")
+                    for i in range(TILES_PER_BANK):
+                        nc.tensor.matmul(
+                            out_ps[:, i, :], weights_flip[:, i, :], v_t[:, first + i, :], start=True, stop=True
+                        )
+                    inv_sum = stats.tile([T, TILES_PER_BANK], F32, name="inv_sum")
+                    nc.vector.reciprocal(inv_sum[:], row_sum[:])
+                    nc.vector.tensor_tensor(
+                        staged[:, first : first + TILES_PER_BANK, :],
+                        out_ps[:],
+                        inv_sum[:].unsqueeze(2).to_broadcast([T, TILES_PER_BANK, DH]),
+                        op=ALU.mult,
+                    )
+
+                heads = slice(g * HEADS_PER_LOAD, (g + 1) * HEADS_PER_LOAD)
+                nc.scalar.dma_start(out[heads].rearrange("h n t d -> t (h n) d"), staged[:])
+                if g + PREFETCH < N_LOADS:
+                    loaded.append(load_group(g + PREFETCH))

@@ -21,9 +21,11 @@ HEADS_PER_LOAD = 8
 TILES_PER_LOAD = HEADS_PER_LOAD * B
 N_LOADS = NH // HEADS_PER_LOAD
 PREFETCH = 10
+SPLIT_AHEAD = 3
 HEADS_PER_BANK = 2
 TILES_PER_BANK = HEADS_PER_BANK * B
 BANKS_PER_LOAD = TILES_PER_LOAD // TILES_PER_BANK
+N_BANKS = N_LOADS * BANKS_PER_LOAD
 
 
 def tile_flexattentioncpb_b_kernel(tc, rel_table, w1, b1, w2, q, k, v, offs, out):
@@ -31,6 +33,7 @@ def tile_flexattentioncpb_b_kernel(tc, rel_table, w1, b1, w2, q, k, v, offs, out
     with (
         tc.tile_pool(name="held", bufs=1) as held,
         tc.tile_pool(name="inputs", bufs=PREFETCH) as inputs,
+        tc.tile_pool(name="split", bufs=SPLIT_AHEAD) as split,
     ):
         offsets = held.tile([P, N // 16], U16, name="offsets")
         nc.sync.dma_start(offsets[:], offs)
@@ -43,11 +46,11 @@ def tile_flexattentioncpb_b_kernel(tc, rel_table, w1, b1, w2, q, k, v, offs, out
 
         def load_group(g):
             heads = slice(g * HEADS_PER_LOAD, (g + 1) * HEADS_PER_LOAD)
-            q_t = inputs.tile([DH, TILES_PER_LOAD, T], BF16, name="q_t")
-            k_t = inputs.tile([DH, TILES_PER_LOAD, T], BF16, name="k_t")
+            q_t = inputs.tile([P, HEADS_PER_LOAD, 2 * T], BF16, name="q_t")
+            k_t = inputs.tile([P, HEADS_PER_LOAD, 2 * T], BF16, name="k_t")
             v_t = inputs.tile([T, TILES_PER_LOAD, DH], BF16, name="v_t")
-            nc.sync.dma_start(q_t[:], q[heads].rearrange("h n d t -> d (h n) t"))
-            nc.sync.dma_start(k_t[:], k[heads].rearrange("h n d t -> d (h n) t"))
+            nc.sync.dma_start(q_t[:], q[heads].rearrange("h n (j e) t -> (n j) h (e t)", e=2))
+            nc.sync.dma_start(k_t[:], k[heads].rearrange("h n (j e) t -> (n j) h (e t)", e=2))
             nc.sync.dma_start(v_t[:], v[heads].rearrange("h n u d -> u (h n) d"))
             return q_t, k_t, v_t
 
@@ -60,6 +63,22 @@ def tile_flexattentioncpb_b_kernel(tc, rel_table, w1, b1, w2, q, k, v, offs, out
             pick_a = held.tile([P, 2, PLACES], BF16, name="pick%d" % a)
             nc.vector.tensor_scalar(pick_a[:], diff[:], float(-a), None, op0=ALU.is_equal)
             pick.append(pick_a)
+
+        own = held.tile([P, B], F32, name="own")
+        nc.vector.memset(own[:], 0.0)
+        for n in range(B):
+            nc.vector.memset(own[n * 64 : (n + 1) * 64, n : n + 1], 1.0)
+
+        loaded = []
+        k_split_of = []
+
+        def split_k(g):
+            k_split = split.tile([P, HEADS_PER_LOAD, B, 2 * T], BF16, name="k_split")
+            for n in range(B):
+                nc.gpsimd.tensor_scalar(
+                    k_split[:, :, n, :], loaded[g][1][:], own[:, n : n + 1], 0.0, op0=ALU.mult, op1=ALU.add
+                )
+            k_split_of.append(k_split)
 
         hid_t = held.tile([HID, ROWS], BF16, name="hid_t")
         bias_x = held.tile([P, NH, HALF], BF16, name="bias_x")
@@ -77,7 +96,10 @@ def tile_flexattentioncpb_b_kernel(tc, rel_table, w1, b1, w2, q, k, v, offs, out
                 )
                 rel_parts.append(rel_c)
 
-            loaded = [load_group(g) for g in range(PREFETCH)]
+            for g in range(PREFETCH):
+                loaded.append(load_group(g))
+            for g in range(SPLIT_AHEAD):
+                split_k(g)
 
             for c in range(3):
                 flipped = setup_psum.tile([P, 8, P], BF16, name="flipped")
@@ -120,85 +142,133 @@ def tile_flexattentioncpb_b_kernel(tc, rel_table, w1, b1, w2, q, k, v, offs, out
                     nc.scalar.copy(bias_x[:, :, blk * 8 : (blk + 1) * 8], by_head)
 
         with (
-            tc.tile_pool(name="work", bufs=3) as work,
-            tc.tile_pool(name="stats", bufs=4) as stats,
+            tc.tile_pool(name="work", bufs=4) as work,
+            tc.tile_pool(name="stats", bufs=6) as stats,
             tc.tile_pool(name="staging", bufs=2) as staging,
-            tc.psum_pool(name="score_psum", bufs=3) as score_psum,
+            tc.psum_pool(name="score_psum", bufs=4) as score_psum,
             tc.psum_pool(name="flip_psum", bufs=2) as flip_psum,
-            tc.psum_pool(name="out_psum", bufs=3) as out_psum,
+            tc.psum_pool(name="out_psum", bufs=2) as out_psum,
         ):
-            for g in range(N_LOADS):
-                q_t, k_t, v_t = loaded[g]
-                staged = staging.tile([T, TILES_PER_LOAD, DH], F32, name="staged")
-                for bank in range(BANKS_PER_LOAD):
-                    first = bank * TILES_PER_BANK
-                    head = g * HEADS_PER_LOAD + bank * HEADS_PER_BANK
+            staged_of = [None] * N_LOADS
+            scores_of = [None] * N_BANKS
+            shift_of = [None] * N_BANKS
+            weights_of = [None] * N_BANKS
+            row_sum_of = [None] * N_BANKS
+            flip_ps_of = [None] * N_BANKS
+            weights_flip_of = [None] * N_BANKS
+            out_ps_of = [None] * N_BANKS
 
-                    scores = score_psum.tile([T, BANK], F32, name="scores")
-                    by_half = scores[:].rearrange(
-                        "t (h r a c) -> t h r a c", h=HEADS_PER_BANK, r=2 * B, a=2
+            def score_matmuls(b):
+                g, bank = divmod(b, BANKS_PER_LOAD)
+                q_t = loaded[g][0]
+                k_split = k_split_of[g]
+                head = b * HEADS_PER_BANK
+                scores = score_psum.tile([T, BANK], F32, name="scores")
+                by_half = scores[:].rearrange("t (h r a c) -> t h r a c", h=HEADS_PER_BANK, r=2 * B, a=2)
+                for a in range(2):
+                    nc.tensor.matmul(
+                        by_half[:, :, :, a, :],
+                        pick[a][:].rearrange("m f t -> m (f t)"),
+                        bias_x[:, head : head + HEADS_PER_BANK, :]
+                        .unsqueeze(2)
+                        .to_broadcast([P, HEADS_PER_BANK, 2 * B, HALF]),
+                        start=(a == 0),
+                        stop=False,
                     )
-                    for a in range(2):
+                by_head = scores[:].rearrange("t (h n u) -> t h n u", h=HEADS_PER_BANK, n=B)
+                for hb in range(HEADS_PER_BANK):
+                    hl = bank * HEADS_PER_BANK + hb
+                    for e in range(2):
                         nc.tensor.matmul(
-                            by_half[:, :, :, a, :],
-                            pick[a][:].rearrange("m f t -> m (f t)"),
-                            bias_x[:, head : head + HEADS_PER_BANK, :]
-                            .unsqueeze(2)
-                            .to_broadcast([P, HEADS_PER_BANK, 2 * B, HALF]),
-                            start=(a == 0),
-                            stop=False,
-                        )
-                    for i in range(TILES_PER_BANK):
-                        nc.tensor.matmul(
-                            scores[:, i * T : (i + 1) * T],
-                            q_t[:, first + i, :],
-                            k_t[:, first + i, :],
+                            by_head[:, hb, :, :],
+                            q_t[:, hl, e * T : (e + 1) * T],
+                            k_split[:, hl, :, e * T : (e + 1) * T],
                             start=False,
-                            stop=(i == TILES_PER_BANK - 1),
+                            stop=(hb == HEADS_PER_BANK - 1 and e == 1),
                         )
+                scores_of[b] = scores
+                if bank == BANKS_PER_LOAD - 1 and g + SPLIT_AHEAD < N_LOADS:
+                    split_k(g + SPLIT_AHEAD)
 
-                    row_max = stats.tile([T, TILES_PER_BANK], F32, name="row_max")
-                    nc.vector.tensor_reduce(
-                        row_max[:],
-                        scores[:].rearrange("t (i u) -> t i u", i=TILES_PER_BANK),
-                        axis=mybir.AxisListType.X,
-                        op=ALU.max,
+            def row_maxima(b):
+                row_max = stats.tile([T, TILES_PER_BANK], F32, name="row_max")
+                nc.vector.tensor_reduce(
+                    row_max[:],
+                    scores_of[b][:].rearrange("t (i u) -> t i u", i=TILES_PER_BANK),
+                    axis=mybir.AxisListType.X,
+                    op=ALU.max,
+                )
+                shift = stats.tile([T, TILES_PER_BANK], F32, name="shift")
+                nc.vector.tensor_scalar(shift[:], row_max[:], -SCALE, None, op0=ALU.mult)
+                shift_of[b] = shift
+
+            def exponentials(b):
+                weights = work.tile([T, TILES_PER_BANK, T], BF16, name="weights")
+                row_sum = stats.tile([T, TILES_PER_BANK], F32, name="row_sum")
+                for i in range(TILES_PER_BANK):
+                    nc.scalar.activation(
+                        weights[:, i, :],
+                        scores_of[b][:, i * T : (i + 1) * T],
+                        ACT.Exp,
+                        bias=shift_of[b][:, i : i + 1],
+                        scale=SCALE,
+                        accum_out=row_sum[:, i : i + 1],
                     )
-                    shift = stats.tile([T, TILES_PER_BANK], F32, name="shift")
-                    nc.vector.tensor_scalar(shift[:], row_max[:], -SCALE, None, op0=ALU.mult)
-                    weights = work.tile([T, TILES_PER_BANK, T], BF16, name="weights")
-                    row_sum = stats.tile([T, TILES_PER_BANK], F32, name="row_sum")
-                    for i in range(TILES_PER_BANK):
-                        nc.scalar.activation(
-                            weights[:, i, :],
-                            scores[:, i * T : (i + 1) * T],
-                            ACT.Exp,
-                            bias=shift[:, i : i + 1],
-                            scale=SCALE,
-                            accum_out=row_sum[:, i : i + 1],
-                        )
+                weights_of[b] = weights
+                row_sum_of[b] = row_sum
 
-                    flip_ps = flip_psum.tile([T, TILES_PER_BANK, T], BF16, name="flip_ps")
-                    for i in range(TILES_PER_BANK):
-                        nc.tensor.transpose(flip_ps[:, i, :], weights[:, i, :], ident[:])
-                    weights_flip = work.tile([T, TILES_PER_BANK, T], BF16, name="weights_flip")
-                    nc.scalar.copy(weights_flip[:], flip_ps[:])
+            def flips(b):
+                flip_ps = flip_psum.tile([T, TILES_PER_BANK, T], BF16, name="flip_ps")
+                for i in range(TILES_PER_BANK):
+                    nc.tensor.transpose(flip_ps[:, i, :], weights_of[b][:, i, :], ident[:])
+                flip_ps_of[b] = flip_ps
 
-                    out_ps = out_psum.tile([T, TILES_PER_BANK, DH], F32, name="out_ps")
-                    for i in range(TILES_PER_BANK):
-                        nc.tensor.matmul(
-                            out_ps[:, i, :], weights_flip[:, i, :], v_t[:, first + i, :], start=True, stop=True
-                        )
-                    inv_sum = stats.tile([T, TILES_PER_BANK], F32, name="inv_sum")
-                    nc.vector.reciprocal(inv_sum[:], row_sum[:])
-                    nc.vector.tensor_tensor(
-                        staged[:, first : first + TILES_PER_BANK, :],
-                        out_ps[:],
-                        inv_sum[:].unsqueeze(2).to_broadcast([T, TILES_PER_BANK, DH]),
-                        op=ALU.mult,
+            def flip_copy(b):
+                weights_flip = work.tile([T, TILES_PER_BANK, T], BF16, name="weights_flip")
+                nc.scalar.copy(weights_flip[:], flip_ps_of[b][:])
+                weights_flip_of[b] = weights_flip
+
+            def value_matmuls(b):
+                g, bank = divmod(b, BANKS_PER_LOAD)
+                v_t = loaded[g][2]
+                out_ps = out_psum.tile([T, TILES_PER_BANK, DH], F32, name="out_ps")
+                for i in range(TILES_PER_BANK):
+                    nc.tensor.matmul(
+                        out_ps[:, i, :],
+                        weights_flip_of[b][:, i, :],
+                        v_t[:, bank * TILES_PER_BANK + i, :],
+                        start=True,
+                        stop=True,
                     )
-
-                heads = slice(g * HEADS_PER_LOAD, (g + 1) * HEADS_PER_LOAD)
-                nc.scalar.dma_start(out[heads].rearrange("h n t d -> t (h n) d"), staged[:])
-                if g + PREFETCH < N_LOADS:
+                out_ps_of[b] = out_ps
+                if bank == BANKS_PER_LOAD - 1 and g + PREFETCH < N_LOADS:
                     loaded.append(load_group(g + PREFETCH))
+
+            def normalise(b):
+                g, bank = divmod(b, BANKS_PER_LOAD)
+                if bank == 0:
+                    staged_of[g] = staging.tile([T, TILES_PER_LOAD, DH], F32, name="staged")
+                inv_sum = stats.tile([T, TILES_PER_BANK], F32, name="inv_sum")
+                nc.vector.reciprocal(inv_sum[:], row_sum_of[b][:])
+                nc.vector.tensor_tensor(
+                    staged_of[g][:, bank * TILES_PER_BANK : (bank + 1) * TILES_PER_BANK, :],
+                    out_ps_of[b][:],
+                    inv_sum[:].unsqueeze(2).to_broadcast([T, TILES_PER_BANK, DH]),
+                    op=ALU.mult,
+                )
+                if bank == BANKS_PER_LOAD - 1:
+                    heads = slice(g * HEADS_PER_LOAD, (g + 1) * HEADS_PER_LOAD)
+                    nc.sync.dma_start(out[heads].rearrange("h n t d -> t (h n) d"), staged_of[g][:])
+
+            def run(stage, b):
+                if 0 <= b < N_BANKS:
+                    stage(b)
+
+            for s in range(N_BANKS + 6):
+                run(score_matmuls, s)
+                run(row_maxima, s - 1)
+                run(exponentials, s - 2)
+                run(flips, s - 3)
+                run(flip_copy, s - 4)
+                run(value_matmuls, s - 5)
+                run(normalise, s - 6)

@@ -21,7 +21,6 @@ HEADS_PER_LOAD = 8
 TILES_PER_LOAD = HEADS_PER_LOAD * B
 N_LOADS = NH // HEADS_PER_LOAD
 PREFETCH = 10
-SPLIT_AHEAD = 3
 HEADS_PER_BANK = 2
 TILES_PER_BANK = HEADS_PER_BANK * B
 BANKS_PER_LOAD = TILES_PER_LOAD // TILES_PER_BANK
@@ -33,7 +32,6 @@ def tile_flexattentioncpb_b_kernel(tc, rel_table, w1, b1, w2, q, k, v, offs, out
     with (
         tc.tile_pool(name="held", bufs=1) as held,
         tc.tile_pool(name="inputs", bufs=PREFETCH) as inputs,
-        tc.tile_pool(name="split", bufs=SPLIT_AHEAD) as split,
     ):
         offsets = held.tile([P, N // 16], U16, name="offsets")
         nc.sync.dma_start(offsets[:], offs)
@@ -47,12 +45,13 @@ def tile_flexattentioncpb_b_kernel(tc, rel_table, w1, b1, w2, q, k, v, offs, out
         def load_group(g):
             heads = slice(g * HEADS_PER_LOAD, (g + 1) * HEADS_PER_LOAD)
             q_t = inputs.tile([P, HEADS_PER_LOAD, 2 * T], BF16, name="q_t")
-            k_t = inputs.tile([P, HEADS_PER_LOAD, 2 * T], BF16, name="k_t")
+            k_split = k_split_ring[g % PREFETCH]
             v_t = inputs.tile([T, TILES_PER_LOAD, DH], BF16, name="v_t")
-            nc.sync.dma_start(q_t[:], q[heads].rearrange("h n (j e) t -> (n j) h (e t)", e=2))
-            nc.sync.dma_start(k_t[:], k[heads].rearrange("h n (j e) t -> (n j) h (e t)", e=2))
+            for n in range(B):
+                nc.sync.dma_start(q_t[n::2, :, :], q[heads, n].rearrange("h (j e) t -> j h (e t)", e=2))
+                nc.sync.dma_start(k_split[n::2, :, n, :], k[heads, n].rearrange("h (j e) t -> j h (e t)", e=2))
             nc.sync.dma_start(v_t[:], v[heads].rearrange("h n u d -> u (h n) d"))
-            return q_t, k_t, v_t
+            return q_t, k_split, v_t
 
         ident = held.tile([P, P], BF16, name="ident")
         make_identity(nc, ident[:])
@@ -64,21 +63,13 @@ def tile_flexattentioncpb_b_kernel(tc, rel_table, w1, b1, w2, q, k, v, offs, out
             nc.vector.tensor_scalar(pick_a[:], diff[:], float(-a), None, op0=ALU.is_equal)
             pick.append(pick_a)
 
-        own = held.tile([P, B], F32, name="own")
-        nc.vector.memset(own[:], 0.0)
-        for n in range(B):
-            nc.vector.memset(own[n * 64 : (n + 1) * 64, n : n + 1], 1.0)
+        k_split_ring = []
+        for i in range(PREFETCH):
+            k_split = held.tile([P, HEADS_PER_LOAD, B, 2 * T], BF16, name="k_split%d" % i)
+            nc.gpsimd.memset(k_split[:].bitcast(F32), 0.0)
+            k_split_ring.append(k_split)
 
         loaded = []
-        k_split_of = []
-
-        def split_k(g):
-            k_split = split.tile([P, HEADS_PER_LOAD, B, 2 * T], BF16, name="k_split")
-            for n in range(B):
-                nc.gpsimd.tensor_scalar(
-                    k_split[:, :, n, :], loaded[g][1][:], own[:, n : n + 1], 0.0, op0=ALU.mult, op1=ALU.add
-                )
-            k_split_of.append(k_split)
 
         hid_t = held.tile([HID, ROWS], BF16, name="hid_t")
         bias_x = held.tile([P, NH, HALF], BF16, name="bias_x")
@@ -98,8 +89,6 @@ def tile_flexattentioncpb_b_kernel(tc, rel_table, w1, b1, w2, q, k, v, offs, out
 
             for g in range(PREFETCH):
                 loaded.append(load_group(g))
-            for g in range(SPLIT_AHEAD):
-                split_k(g)
 
             for c in range(3):
                 flipped = setup_psum.tile([P, 8, P], BF16, name="flipped")
@@ -161,7 +150,7 @@ def tile_flexattentioncpb_b_kernel(tc, rel_table, w1, b1, w2, q, k, v, offs, out
             def score_matmuls(b):
                 g, bank = divmod(b, BANKS_PER_LOAD)
                 q_t = loaded[g][0]
-                k_split = k_split_of[g]
+                k_split = loaded[g][1]
                 head = b * HEADS_PER_BANK
                 scores = score_psum.tile([T, BANK], F32, name="scores")
                 by_half = scores[:].rearrange("t (h r a c) -> t h r a c", h=HEADS_PER_BANK, r=2 * B, a=2)
@@ -187,8 +176,6 @@ def tile_flexattentioncpb_b_kernel(tc, rel_table, w1, b1, w2, q, k, v, offs, out
                             stop=(hb == HEADS_PER_BANK - 1 and e == 1),
                         )
                 scores_of[b] = scores
-                if bank == BANKS_PER_LOAD - 1 and g + SPLIT_AHEAD < N_LOADS:
-                    split_k(g + SPLIT_AHEAD)
 
             def row_maxima(b):
                 row_max = stats.tile([T, TILES_PER_BANK], F32, name="row_max")

@@ -245,7 +245,7 @@ def tile_flexattentioncpb_b_kernel(tc, rel_table, w1, b1, w2, q, k, v, offs, out
                 )
                 if bank == BANKS_PER_LOAD - 1:
                     heads = slice(g * HEADS_PER_LOAD, (g + 1) * HEADS_PER_LOAD)
-                    nc.sync.dma_start(out[heads].rearrange("h n t d -> t (h n) d"), staged_of[g][:])
+                    nc.scalar.dma_start(out[heads].rearrange("h n t d -> t (h n) d"), staged_of[g][:])
 
             def run(stage, b):
                 if 0 <= b < N_BANKS:

@@ -25,6 +25,8 @@ HEADS_PER_BANK = 2
 TILES_PER_BANK = HEADS_PER_BANK * B
 BANKS_PER_LOAD = TILES_PER_LOAD // TILES_PER_BANK
 N_BANKS = N_LOADS * BANKS_PER_LOAD
+N_PLAIN_LOADS = 12
+N_PAIRED_LOADS = N_LOADS - N_PLAIN_LOADS
 
 
 def tile_flexattentioncpb_b_kernel(tc, rel_table, w1, b1, w2, q, k, v, offs, out):
@@ -45,13 +47,19 @@ def tile_flexattentioncpb_b_kernel(tc, rel_table, w1, b1, w2, q, k, v, offs, out
         def load_group(g):
             heads = slice(g * HEADS_PER_LOAD, (g + 1) * HEADS_PER_LOAD)
             q_t = inputs.tile([P, HEADS_PER_LOAD, 2 * T], BF16, name="q_t")
-            k_split = k_split_ring[g % PREFETCH]
             v_t = inputs.tile([T, TILES_PER_LOAD, DH], BF16, name="v_t")
-            for n in range(B):
-                nc.sync.dma_start(q_t[n::2, :, :], q[heads, n].rearrange("h (j e) t -> j h (e t)", e=2))
-                nc.sync.dma_start(k_split[n::2, :, n, :], k[heads, n].rearrange("h (j e) t -> j h (e t)", e=2))
+            if g < N_PLAIN_LOADS:
+                k_t = inputs.tile([P, HEADS_PER_LOAD, 2 * T], BF16, name="k_t")
+                by_tile = "d h (n t) -> d (h n) t"
+                nc.sync.dma_start(q_t[:].rearrange(by_tile, n=B), q[heads].rearrange("h n d t -> d (h n) t"))
+                nc.sync.dma_start(k_t[:].rearrange(by_tile, n=B), k[heads].rearrange("h n d t -> d (h n) t"))
+            else:
+                k_t = k_split_ring[g - N_PLAIN_LOADS]
+                for n in range(B):
+                    nc.sync.dma_start(q_t[n::2, :, :], q[heads, n].rearrange("h (j e) t -> j h (e t)", e=2))
+                    nc.sync.dma_start(k_t[n::2, :, n, :], k[heads, n].rearrange("h (j e) t -> j h (e t)", e=2))
             nc.sync.dma_start(v_t[:], v[heads].rearrange("h n u d -> u (h n) d"))
-            return q_t, k_split, v_t
+            return q_t, k_t, v_t
 
         ident = held.tile([P, P], BF16, name="ident")
         make_identity(nc, ident[:])
@@ -64,7 +72,7 @@ def tile_flexattentioncpb_b_kernel(tc, rel_table, w1, b1, w2, q, k, v, offs, out
             pick.append(pick_a)
 
         k_split_ring = []
-        for i in range(PREFETCH):
+        for i in range(N_PAIRED_LOADS):
             k_split = held.tile([P, HEADS_PER_LOAD, B, 2 * T], BF16, name="k_split%d" % i)
             nc.gpsimd.memset(k_split[:].bitcast(F32), 0.0)
             k_split_ring.append(k_split)
@@ -150,7 +158,7 @@ def tile_flexattentioncpb_b_kernel(tc, rel_table, w1, b1, w2, q, k, v, offs, out
             def score_matmuls(b):
                 g, bank = divmod(b, BANKS_PER_LOAD)
                 q_t = loaded[g][0]
-                k_split = loaded[g][1]
+                k_t = loaded[g][1]
                 head = b * HEADS_PER_BANK
                 scores = score_psum.tile([T, BANK], F32, name="scores")
                 by_half = scores[:].rearrange("t (h r a c) -> t h r a c", h=HEADS_PER_BANK, r=2 * B, a=2)
@@ -167,14 +175,17 @@ def tile_flexattentioncpb_b_kernel(tc, rel_table, w1, b1, w2, q, k, v, offs, out
                 by_head = scores[:].rearrange("t (h n u) -> t h n u", h=HEADS_PER_BANK, n=B)
                 for hb in range(HEADS_PER_BANK):
                     hl = bank * HEADS_PER_BANK + hb
-                    for e in range(2):
-                        nc.tensor.matmul(
-                            by_head[:, hb, :, :],
-                            q_t[:, hl, e * T : (e + 1) * T],
-                            k_split[:, hl, :, e * T : (e + 1) * T],
-                            start=False,
-                            stop=(hb == HEADS_PER_BANK - 1 and e == 1),
-                        )
+                    for x in range(2):
+                        half = slice(x * T, (x + 1) * T)
+                        last = hb == HEADS_PER_BANK - 1 and x == 1
+                        if g < N_PLAIN_LOADS:
+                            nc.tensor.matmul(
+                                by_head[:, hb, x, :], q_t[:, hl, half], k_t[:, hl, half], start=False, stop=last
+                            )
+                        else:
+                            nc.tensor.matmul(
+                                by_head[:, hb, :, :], q_t[:, hl, half], k_t[:, hl, :, half], start=False, stop=last
+                            )
                 scores_of[b] = scores
 
             def row_maxima(b):

@@ -141,7 +141,7 @@ def tile_flexattentioncpb_b_kernel(tc, rel_table, w1, b1, w2, q, k, v, offs, out
         with (
             tc.tile_pool(name="work", bufs=4) as work,
             tc.tile_pool(name="stats", bufs=6) as stats,
-            tc.tile_pool(name="staging", bufs=2) as staging,
+            tc.tile_pool(name="staging", bufs=4) as staging,
             tc.psum_pool(name="score_psum", bufs=4) as score_psum,
             tc.psum_pool(name="flip_psum", bufs=2) as flip_psum,
             tc.psum_pool(name="out_psum", bufs=2) as out_psum,

@@ -25,7 +25,7 @@ HEADS_PER_BANK = 2
 TILES_PER_BANK = HEADS_PER_BANK * B
 BANKS_PER_LOAD = TILES_PER_LOAD // TILES_PER_BANK
 N_BANKS = N_LOADS * BANKS_PER_LOAD
-N_PLAIN_LOADS = 12
+N_PLAIN_LOADS = 10
 N_PAIRED_LOADS = N_LOADS - N_PLAIN_LOADS
 
 

@@ -3,7 +3,6 @@ from concourse.masks import make_identity
 
 BF16 = mybir.dt.bfloat16
 F32 = mybir.dt.float32
-I32 = mybir.dt.int32
 U16 = mybir.dt.uint16
 ACT = mybir.ActivationFunctionType
 ALU = mybir.AluOpType
@@ -25,8 +24,9 @@ HEADS_PER_BANK = 2
 TILES_PER_BANK = HEADS_PER_BANK * B
 BANKS_PER_LOAD = TILES_PER_LOAD // TILES_PER_BANK
 N_BANKS = N_LOADS * BANKS_PER_LOAD
-N_PLAIN_LOADS = 10
-N_PAIRED_LOADS = N_LOADS - N_PLAIN_LOADS
+N_PLAIN_LOADS = 8
+N_SPLIT_TILES = 6
+FIRST_REUSE = N_PLAIN_LOADS + N_SPLIT_TILES
 
 
 def tile_flexattentioncpb_b_kernel(tc, rel_table, w1, b1, w2, q, k, v, offs, out):
@@ -49,12 +49,12 @@ def tile_flexattentioncpb_b_kernel(tc, rel_table, w1, b1, w2, q, k, v, offs, out
             q_t = inputs.tile([P, HEADS_PER_LOAD, 2 * T], BF16, name="q_t")
             v_t = inputs.tile([T, TILES_PER_LOAD, DH], BF16, name="v_t")
             if g < N_PLAIN_LOADS:
-                k_t = inputs.tile([P, HEADS_PER_LOAD, 2 * T], BF16, name="k_t")
+                k_t = inputs.tile([P, HEADS_PER_LOAD, 2 * T], BF16, name="k_t", bufs=N_PLAIN_LOADS)
                 by_tile = "d h (n t) -> d (h n) t"
                 nc.sync.dma_start(q_t[:].rearrange(by_tile, n=B), q[heads].rearrange("h n d t -> d (h n) t"))
                 nc.sync.dma_start(k_t[:].rearrange(by_tile, n=B), k[heads].rearrange("h n d t -> d (h n) t"))
             else:
-                k_t = k_split_ring[g - N_PLAIN_LOADS]
+                k_t = k_split_ring[(g - N_PLAIN_LOADS) % N_SPLIT_TILES]
                 for n in range(B):
                     nc.sync.dma_start(q_t[n::2, :, :], q[heads, n].rearrange("h (j e) t -> j h (e t)", e=2))
                     nc.sync.dma_start(k_t[n::2, :, n, :], k[heads, n].rearrange("h (j e) t -> j h (e t)", e=2))
@@ -63,16 +63,23 @@ def tile_flexattentioncpb_b_kernel(tc, rel_table, w1, b1, w2, q, k, v, offs, out
 
         ident = held.tile([P, P], BF16, name="ident")
         make_identity(nc, ident[:])
-        diff = held.tile([P, 2, PLACES], I32, name="diff")
-        nc.gpsimd.iota(diff[:], pattern=[[0, 2], [2, PLACES]], base=0, channel_multiplier=-1)
         pick = []
         for a in range(2):
             pick_a = held.tile([P, 2, PLACES], BF16, name="pick%d" % a)
-            nc.vector.tensor_scalar(pick_a[:], diff[:], float(-a), None, op0=ALU.is_equal)
+            nc.gpsimd.memset(pick_a[:], 0.0)
+            nc.gpsimd.affine_select(
+                out=pick_a[:],
+                in_=pick_a[:],
+                compare_op=ALU.not_equal,
+                fill=1.0,
+                base=a,
+                pattern=[[0, 2], [2, PLACES]],
+                channel_multiplier=-1,
+            )
             pick.append(pick_a)
 
         k_split_ring = []
-        for i in range(N_PAIRED_LOADS):
+        for i in range(N_SPLIT_TILES):
             k_split = held.tile([P, HEADS_PER_LOAD, B, 2 * T], BF16, name="k_split%d" % i)
             nc.gpsimd.memset(k_split[:].bitcast(F32), 0.0)
             k_split_ring.append(k_split)
@@ -187,6 +194,8 @@ def tile_flexattentioncpb_b_kernel(tc, rel_table, w1, b1, w2, q, k, v, offs, out
                                 by_head[:, hb, :, :], q_t[:, hl, half], k_t[:, hl, :, half], start=False, stop=last
                             )
                 scores_of[b] = scores
+                if bank == BANKS_PER_LOAD - 1 and FIRST_REUSE <= g + N_SPLIT_TILES < N_LOADS:
+                    loaded.append(load_group(g + N_SPLIT_TILES))
 
             def row_maxima(b):
                 row_max = stats.tile([T, TILES_PER_BANK], F32, name="row_max")
@@ -239,7 +248,7 @@ def tile_flexattentioncpb_b_kernel(tc, rel_table, w1, b1, w2, q, k, v, offs, out
                         stop=True,
                     )
                 out_ps_of[b] = out_ps
-                if bank == BANKS_PER_LOAD - 1 and g + PREFETCH < N_LOADS:
+                if bank == BANKS_PER_LOAD - 1 and g + PREFETCH < FIRST_REUSE:
                     loaded.append(load_group(g + PREFETCH))
 
             def normalise(b):

@@ -24,7 +24,7 @@ HEADS_PER_BANK = 2
 TILES_PER_BANK = HEADS_PER_BANK * B
 BANKS_PER_LOAD = TILES_PER_LOAD // TILES_PER_BANK
 N_BANKS = N_LOADS * BANKS_PER_LOAD
-N_PLAIN_LOADS = 8
+N_PLAIN_LOADS = 6
 N_SPLIT_TILES = 6
 FIRST_REUSE = N_PLAIN_LOADS + N_SPLIT_TILES
 

@@ -138,7 +138,7 @@ def tile_flexattentioncpb_b_kernel(tc, rel_table, w1, b1, w2, q, k, v, offs, out
             for blk in range(HALF // 8):
                 flipped = setup_psum.tile([P, 8, P], BF16, name="flipped")
                 for c in range(8):
-                    nc.tensor.transpose(flipped[:, c, :], bias_h[:, :, blk * 8 + c], ident[:])
+                    nc.tensor.matmul(flipped[:, c, :], bias_h[:, :, blk * 8 + c], ident[:], start=True, stop=True)
                 by_head = flipped[:].rearrange("m c h -> m h c")
                 if blk % 2 == 0:
                     nc.vector.tensor_copy(bias_x[:, :, blk * 8 : (blk + 1) * 8], by_head)

@@ -24,7 +24,7 @@ HEADS_PER_BANK = 2
 TILES_PER_BANK = HEADS_PER_BANK * B
 BANKS_PER_LOAD = TILES_PER_LOAD // TILES_PER_BANK
 N_BANKS = N_LOADS * BANKS_PER_LOAD
-N_PLAIN_LOADS = 6
+N_PLAIN_LOADS = 5
 N_SPLIT_TILES = 6
 FIRST_REUSE = N_PLAIN_LOADS + N_SPLIT_TILES
 
@@ -34,7 +34,11 @@ def tile_flexattentioncpb_b_kernel(tc, rel_table, w1, b1, w2, q, k, v, offs, out
     with (
         tc.tile_pool(name="held", bufs=1) as held,
         tc.tile_pool(name="inputs", bufs=PREFETCH) as inputs,
+        tc.psum_pool(name="psum", bufs=2) as psum,
     ):
+        def wide_bank(name):
+            return psum.tile([P, BANK], F32, name=name, tag="wide", bufs=4)
+
         offsets = held.tile([P, N // 16], U16, name="offsets")
         nc.sync.dma_start(offsets[:], offs)
         w1_t = held.tile([CF, HID], BF16, name="w1_t")
@@ -63,20 +67,24 @@ def tile_flexattentioncpb_b_kernel(tc, rel_table, w1, b1, w2, q, k, v, offs, out
 
         ident = held.tile([P, P], BF16, name="ident")
         make_identity(nc, ident[:])
-        pick = []
+        pick = held.tile([P, 2, PLACES], BF16, name="pick")
+        nc.gpsimd.memset(pick[:], 0.0)
         for a in range(2):
-            pick_a = held.tile([P, 2, PLACES], BF16, name="pick%d" % a)
-            nc.gpsimd.memset(pick_a[:], 0.0)
             nc.gpsimd.affine_select(
-                out=pick_a[:],
-                in_=pick_a[:],
+                out=pick[:],
+                in_=pick[:],
                 compare_op=ALU.not_equal,
                 fill=1.0,
                 base=a,
                 pattern=[[0, 2], [2, PLACES]],
                 channel_multiplier=-1,
             )
-            pick.append(pick_a)
+        is_half = []
+        for a in range(2):
+            is_half_a = held.tile([P, 1], F32, name="is_half%d" % a)
+            columns = held.tile([P, PLACES], BF16, name="columns%d" % a)
+            nc.scalar.activation(columns[:], ident[:, a::2], ACT.Copy, accum_out=is_half_a[:])
+            is_half.append(is_half_a)
 
         k_split_ring = []
         for i in range(N_SPLIT_TILES):
@@ -87,12 +95,9 @@ def tile_flexattentioncpb_b_kernel(tc, rel_table, w1, b1, w2, q, k, v, offs, out
         loaded = []
 
         hid_t = held.tile([HID, ROWS], BF16, name="hid_t")
-        bias_x = held.tile([P, NH, HALF], BF16, name="bias_x")
+        bias_z = held.tile([P, NH, 2, HALF], BF16, name="bias_z")
 
-        with (
-            tc.tile_pool(name="setup", bufs=1) as setup,
-            tc.psum_pool(name="setup_psum", bufs=2) as setup_psum,
-        ):
+        with tc.tile_pool(name="setup", bufs=1) as setup:
             rel_flip = setup.tile([CF, ROWS], BF16, name="rel_flip")
             rel_parts = []
             for c in range(3):
@@ -106,7 +111,7 @@ def tile_flexattentioncpb_b_kernel(tc, rel_table, w1, b1, w2, q, k, v, offs, out
                 loaded.append(load_group(g))
 
             for c in range(3):
-                flipped = setup_psum.tile([P, 8, P], BF16, name="flipped")
+                flipped = psum.tile([P, 8, P], BF16, name="flipped", tag="flip")
                 for a in range(8):
                     nc.tensor.transpose(flipped[:, a, :], rel_parts[c][:, a, :], ident[:])
                 nc.vector.tensor_copy(
@@ -114,14 +119,14 @@ def tile_flexattentioncpb_b_kernel(tc, rel_table, w1, b1, w2, q, k, v, offs, out
                 )
             for blk in range(ROWS // BANK):
                 cols = slice(blk * BANK, (blk + 1) * BANK)
-                hid_ps = setup_psum.tile([P, BANK], F32, name="hid_ps", tag="product", bufs=4)
+                hid_ps = wide_bank("hid_ps")
                 nc.tensor.matmul(hid_ps[:], w1_t[:], rel_flip[:, cols], start=True, stop=True)
                 nc.scalar.activation(hid_t[:, cols], hid_ps[:], ACT.Gelu, bias=b1_t[:, 0:1])
 
             bias_h = setup.tile([NH, P, HALF], BF16, name="bias_h")
             bias_flat = bias_h[:].rearrange("h m c -> h (m c)")
             for piece in range(N // PIECE):
-                bias_ps = setup_psum.tile([P, PIECE], F32, name="bias_ps", tag="product", bufs=4)
+                bias_ps = wide_bank("bias_ps")
                 nc.tensor.matmul(
                     bias_ps[:],
                     w2_t[:],
@@ -136,22 +141,21 @@ def tile_flexattentioncpb_b_kernel(tc, rel_table, w1, b1, w2, q, k, v, offs, out
                     nc.vector.tensor_scalar(bias_flat[:, cols], bias_ps[:], 1.0 / SCALE, None, op0=ALU.mult)
 
             for blk in range(HALF // 8):
-                flipped = setup_psum.tile([P, 8, P], BF16, name="flipped")
+                flipped = psum.tile([P, 8, P], BF16, name="flipped", tag="flip")
                 for c in range(8):
                     nc.tensor.matmul(flipped[:, c, :], bias_h[:, :, blk * 8 + c], ident[:], start=True, stop=True)
                 by_head = flipped[:].rearrange("m c h -> m h c")
-                if blk % 2 == 0:
-                    nc.vector.tensor_copy(bias_x[:, :, blk * 8 : (blk + 1) * 8], by_head)
-                else:
-                    nc.scalar.copy(bias_x[:, :, blk * 8 : (blk + 1) * 8], by_head)
+                for a in range(2):
+                    block = bias_z[:, :, a, blk * 8 : (blk + 1) * 8]
+                    if blk % 2 == 0:
+                        nc.vector.tensor_scalar(block, by_head, is_half[a][:, 0:1], None, op0=ALU.mult)
+                    else:
+                        nc.scalar.activation(block, by_head, ACT.Copy, scale=is_half[a][:, 0:1])
 
         with (
             tc.tile_pool(name="work", bufs=4) as work,
             tc.tile_pool(name="stats", bufs=6) as stats,
             tc.tile_pool(name="staging", bufs=4) as staging,
-            tc.psum_pool(name="score_psum", bufs=4) as score_psum,
-            tc.psum_pool(name="flip_psum", bufs=2) as flip_psum,
-            tc.psum_pool(name="out_psum", bufs=2) as out_psum,
         ):
             staged_of = [None] * N_LOADS
             scores_of = [None] * N_BANKS
@@ -167,32 +171,31 @@ def tile_flexattentioncpb_b_kernel(tc, rel_table, w1, b1, w2, q, k, v, offs, out
                 q_t = loaded[g][0]
                 k_t = loaded[g][1]
                 head = b * HEADS_PER_BANK
-                scores = score_psum.tile([T, BANK], F32, name="scores")
-                by_half = scores[:].rearrange("t (h r a c) -> t h r a c", h=HEADS_PER_BANK, r=2 * B, a=2)
-                for a in range(2):
-                    nc.tensor.matmul(
-                        by_half[:, :, :, a, :],
-                        pick[a][:].rearrange("m f t -> m (f t)"),
-                        bias_x[:, head : head + HEADS_PER_BANK, :]
-                        .unsqueeze(2)
-                        .to_broadcast([P, HEADS_PER_BANK, 2 * B, HALF]),
-                        start=(a == 0),
-                        stop=False,
-                    )
+                scores = wide_bank("scores")
                 by_head = scores[:].rearrange("t (h n u) -> t h n u", h=HEADS_PER_BANK, n=B)
                 for hb in range(HEADS_PER_BANK):
                     hl = bank * HEADS_PER_BANK + hb
                     for x in range(2):
                         half = slice(x * T, (x + 1) * T)
-                        last = hb == HEADS_PER_BANK - 1 and x == 1
+                        first = hb == 0 and x == 0
                         if g < N_PLAIN_LOADS:
                             nc.tensor.matmul(
-                                by_head[:, hb, x, :], q_t[:, hl, half], k_t[:, hl, half], start=False, stop=last
+                                by_head[:, hb, x, :], q_t[:, hl, half], k_t[:, hl, half], start=first, stop=False
                             )
                         else:
                             nc.tensor.matmul(
-                                by_head[:, hb, :, :], q_t[:, hl, half], k_t[:, hl, :, half], start=False, stop=last
+                                by_head[:, hb, :, :], q_t[:, hl, half], k_t[:, hl, :, half], start=first, stop=False
                             )
+                nc.tensor.matmul(
+                    scores[:].rearrange("t (h r u) -> t h r u", h=HEADS_PER_BANK, r=2 * B),
+                    pick[:].rearrange("m f t -> m (f t)"),
+                    bias_z[:, head : head + HEADS_PER_BANK, :, :]
+                    .rearrange("m h a c -> m h (a c)")
+                    .unsqueeze(2)
+                    .to_broadcast([P, HEADS_PER_BANK, 2 * B, PLACES]),
+                    start=False,
+                    stop=True,
+                )
                 scores_of[b] = scores
                 if bank == BANKS_PER_LOAD - 1 and FIRST_REUSE <= g + N_SPLIT_TILES < N_LOADS:
                     loaded.append(load_group(g + N_SPLIT_TILES))
@@ -225,7 +228,7 @@ def tile_flexattentioncpb_b_kernel(tc, rel_table, w1, b1, w2, q, k, v, offs, out
                 row_sum_of[b] = row_sum
 
             def flips(b):
-                flip_ps = flip_psum.tile([T, TILES_PER_BANK, T], BF16, name="flip_ps")
+                flip_ps = psum.tile([T, TILES_PER_BANK, T], BF16, name="flip_ps", tag="flip")
                 for i in range(TILES_PER_BANK):
                     nc.tensor.transpose(flip_ps[:, i, :], weights_of[b][:, i, :], ident[:])
                 flip_ps_of[b] = flip_ps
@@ -238,7 +241,7 @@ def tile_flexattentioncpb_b_kernel(tc, rel_table, w1, b1, w2, q, k, v, offs, out
             def value_matmuls(b):
                 g, bank = divmod(b, BANKS_PER_LOAD)
                 v_t = loaded[g][2]
-                out_ps = out_psum.tile([T, TILES_PER_BANK, DH], F32, name="out_ps")
+                out_ps = psum.tile([T, TILES_PER_BANK, DH], F32, name="out_ps", tag="out")
                 for i in range(TILES_PER_BANK):
                     nc.tensor.matmul(
                         out_ps[:, i, :],
@@ -263,7 +266,11 @@ def tile_flexattentioncpb_b_kernel(tc, rel_table, w1, b1, w2, q, k, v, offs, out
                     inv_sum[:].unsqueeze(2).to_broadcast([T, TILES_PER_BANK, DH]),
                     op=ALU.mult,
                 )
-                if bank == BANKS_PER_LOAD - 1:
+                if g == N_LOADS - 1:
+                    heads = slice(b * HEADS_PER_BANK, (b + 1) * HEADS_PER_BANK)
+                    tiles = slice(bank * TILES_PER_BANK, (bank + 1) * TILES_PER_BANK)
+                    nc.scalar.dma_start(out[heads].rearrange("h n t d -> t (h n) d"), staged_of[g][:, tiles, :])
+                elif bank == BANKS_PER_LOAD - 1:
                     heads = slice(g * HEADS_PER_LOAD, (g + 1) * HEADS_PER_LOAD)
                     nc.scalar.dma_start(out[heads].rearrange("h n t d -> t (h n) d"), staged_of[g][:])
 

import concourse.mybir as mybir
from concourse.masks import make_identity

BF16 = mybir.dt.bfloat16
F32 = mybir.dt.float32
U16 = mybir.dt.uint16
ACT = mybir.ActivationFunctionType
ALU = mybir.AluOpType

P = 128
ROWS, CF, HID, NH, B, T, DH, PLACES, N = 3072, 128, 128, 128, 2, 128, 128, 64, 4096
SCALE = DH**-0.5
FLOPS = 2 * ROWS * CF * HID + 2 * N * HID * NH + 2 * 2 * NH * B * T * T * DH

BANK = 512
PIECE = 512
HALF = 32

HEADS_PER_LOAD = 8
TILES_PER_LOAD = HEADS_PER_LOAD * B
N_LOADS = NH // HEADS_PER_LOAD
PREFETCH = 10
HEADS_PER_BANK = 2
TILES_PER_BANK = HEADS_PER_BANK * B
BANKS_PER_LOAD = TILES_PER_LOAD // TILES_PER_BANK
N_BANKS = N_LOADS * BANKS_PER_LOAD
N_PLAIN_LOADS = 5
N_SPLIT_TILES = 6
FIRST_REUSE = N_PLAIN_LOADS + N_SPLIT_TILES


def tile_flexattentioncpb_b_kernel(tc, rel_table, w1, b1, w2, q, k, v, offs, out):
    nc = tc.nc
    with (
        tc.tile_pool(name="held", bufs=1) as held,
        tc.tile_pool(name="inputs", bufs=PREFETCH) as inputs,
        tc.psum_pool(name="psum", bufs=2) as psum,
    ):
        def wide_bank(name):
            return psum.tile([P, BANK], F32, name=name, tag="wide", bufs=4)

        offsets = held.tile([P, N // 16], U16, name="offsets")
        nc.sync.dma_start(offsets[:], offs)
        w1_t = held.tile([CF, HID], BF16, name="w1_t")
        nc.scalar.dma_start(w1_t[:], w1)
        w2_t = held.tile([HID, NH], BF16, name="w2_t")
        nc.scalar.dma_start(w2_t[:], w2)
        b1_t = held.tile([HID, 1], F32, name="b1_t")
        nc.scalar.dma_start(b1_t[:], b1)

        def load_group(g):
            heads = slice(g * HEADS_PER_LOAD, (g + 1) * HEADS_PER_LOAD)
            q_t = inputs.tile([P, HEADS_PER_LOAD, 2 * T], BF16, name="q_t")
            v_t = inputs.tile([T, TILES_PER_LOAD, DH], BF16, name="v_t")
            if g < N_PLAIN_LOADS:
                k_t = inputs.tile([P, HEADS_PER_LOAD, 2 * T], BF16, name="k_t", bufs=N_PLAIN_LOADS)
                by_tile = "d h (n t) -> d (h n) t"
                nc.sync.dma_start(q_t[:].rearrange(by_tile, n=B), q[heads].rearrange("h n d t -> d (h n) t"))
                nc.sync.dma_start(k_t[:].rearrange(by_tile, n=B), k[heads].rearrange("h n d t -> d (h n) t"))
            else:
                k_t = k_split_ring[(g - N_PLAIN_LOADS) % N_SPLIT_TILES]
                for n in range(B):
                    nc.sync.dma_start(q_t[n::2, :, :], q[heads, n].rearrange("h (j e) t -> j h (e t)", e=2))
                    nc.sync.dma_start(k_t[n::2, :, n, :], k[heads, n].rearrange("h (j e) t -> j h (e t)", e=2))
            nc.sync.dma_start(v_t[:], v[heads].rearrange("h n u d -> u (h n) d"))
            return q_t, k_t, v_t

        ident = held.tile([P, P], BF16, name="ident")
        make_identity(nc, ident[:])
        pick = held.tile([P, 2, PLACES], BF16, name="pick")
        nc.gpsimd.memset(pick[:], 0.0)
        for a in range(2):
            nc.gpsimd.affine_select(
                out=pick[:],
                in_=pick[:],
                compare_op=ALU.not_equal,
                fill=1.0,
                base=a,
                pattern=[[0, 2], [2, PLACES]],
                channel_multiplier=-1,
            )
        is_half = []
        for a in range(2):
            is_half_a = held.tile([P, 1], F32, name="is_half%d" % a)
            columns = held.tile([P, PLACES], BF16, name="columns%d" % a)
            nc.scalar.activation(columns[:], ident[:, a::2], ACT.Copy, accum_out=is_half_a[:])
            is_half.append(is_half_a)

        k_split_ring = []
        for i in range(N_SPLIT_TILES):
            k_split = held.tile([P, HEADS_PER_LOAD, B, 2 * T], BF16, name="k_split%d" % i)
            nc.gpsimd.memset(k_split[:].bitcast(F32), 0.0)
            k_split_ring.append(k_split)

        loaded = []

        hid_t = held.tile([HID, ROWS], BF16, name="hid_t")
        bias_z = held.tile([P, NH, 2, HALF], BF16, name="bias_z")

        with tc.tile_pool(name="setup", bufs=1) as setup:
            rel_flip = setup.tile([CF, ROWS], BF16, name="rel_flip")
            rel_parts = []
            for c in range(3):
                rel_c = setup.tile([P, 8, CF], BF16, name="rel%d" % c)
                nc.sync.dma_start(
                    rel_c[:], rel_table[c * 1024 : (c + 1) * 1024, :].rearrange("(a p) c -> p a c", p=P)
                )
                rel_parts.append(rel_c)

            for g in range(PREFETCH):
                loaded.append(load_group(g))

            for c in range(3):
                flipped = psum.tile([P, 8, P], BF16, name="flipped", tag="flip")
                for a in range(8):
                    nc.tensor.transpose(flipped[:, a, :], rel_parts[c][:, a, :], ident[:])
                nc.vector.tensor_copy(
                    rel_flip[:, c * 1024 : (c + 1) * 1024], flipped[:].rearrange("c a p -> c (a p)")
                )
            for blk in range(ROWS // BANK):
                cols = slice(blk * BANK, (blk + 1) * BANK)
                hid_ps = wide_bank("hid_ps")
                nc.tensor.matmul(hid_ps[:], w1_t[:], rel_flip[:, cols], start=True, stop=True)
                nc.scalar.activation(hid_t[:, cols], hid_ps[:], ACT.Gelu, bias=b1_t[:, 0:1])

            bias_h = setup.tile([NH, P, HALF], BF16, name="bias_h")
            bias_flat = bias_h[:].rearrange("h m c -> h (m c)")
            for piece in range(N // PIECE):
                bias_ps = wide_bank("bias_ps")
                nc.tensor.matmul(
                    bias_ps[:],
                    w2_t[:],
                    hid_t[:].indirect(offsets[:, piece * (PIECE // 16) : (piece + 1) * (PIECE // 16)]),
                    start=True,
                    stop=True,
                )
                cols = slice(piece * PIECE, (piece + 1) * PIECE)
                if piece % 2 == 0:
                    nc.scalar.mul(bias_flat[:, cols], bias_ps[:], 1.0 / SCALE)
                else:
                    nc.vector.tensor_scalar(bias_flat[:, cols], bias_ps[:], 1.0 / SCALE, None, op0=ALU.mult)

            for blk in range(HALF // 8):
                flipped = psum.tile([P, 8, P], BF16, name="flipped", tag="flip")
                for c in range(8):
                    nc.tensor.matmul(flipped[:, c, :], bias_h[:, :, blk * 8 + c], ident[:], start=True, stop=True)
                by_head = flipped[:].rearrange("m c h -> m h c")
                for a in range(2):
                    block = bias_z[:, :, a, blk * 8 : (blk + 1) * 8]
                    if blk % 2 == 0:
                        nc.vector.tensor_scalar(block, by_head, is_half[a][:, 0:1], None, op0=ALU.mult)
                    else:
                        nc.scalar.activation(block, by_head, ACT.Copy, scale=is_half[a][:, 0:1])

        with (
            tc.tile_pool(name="work", bufs=4) as work,
            tc.tile_pool(name="stats", bufs=6) as stats,
            tc.tile_pool(name="staging", bufs=4) as staging,
        ):
            staged_of = [None] * N_LOADS
            scores_of = [None] * N_BANKS
            shift_of = [None] * N_BANKS
            weights_of = [None] * N_BANKS
            row_sum_of = [None] * N_BANKS
            flip_ps_of = [None] * N_BANKS
            weights_flip_of = [None] * N_BANKS
            out_ps_of = [None] * N_BANKS

            def score_matmuls(b):
                g, bank = divmod(b, BANKS_PER_LOAD)
                q_t = loaded[g][0]
                k_t = loaded[g][1]
                head = b * HEADS_PER_BANK
                scores = wide_bank("scores")
                by_head = scores[:].rearrange("t (h n u) -> t h n u", h=HEADS_PER_BANK, n=B)
                for hb in range(HEADS_PER_BANK):
                    hl = bank * HEADS_PER_BANK + hb
                    for x in range(2):
                        half = slice(x * T, (x + 1) * T)
                        first = hb == 0 and x == 0
                        if g < N_PLAIN_LOADS:
                            nc.tensor.matmul(
                                by_head[:, hb, x, :], q_t[:, hl, half], k_t[:, hl, half], start=first, stop=False
                            )
                        else:
                            nc.tensor.matmul(
                                by_head[:, hb, :, :], q_t[:, hl, half], k_t[:, hl, :, half], start=first, stop=False
                            )
                nc.tensor.matmul(
                    scores[:].rearrange("t (h r u) -> t h r u", h=HEADS_PER_BANK, r=2 * B),
                    pick[:].rearrange("m f t -> m (f t)"),
                    bias_z[:, head : head + HEADS_PER_BANK, :, :]
                    .rearrange("m h a c -> m h (a c)")
                    .unsqueeze(2)
                    .to_broadcast([P, HEADS_PER_BANK, 2 * B, PLACES]),
                    start=False,
                    stop=True,
                )
                scores_of[b] = scores
                if bank == BANKS_PER_LOAD - 1 and FIRST_REUSE <= g + N_SPLIT_TILES < N_LOADS:
                    loaded.append(load_group(g + N_SPLIT_TILES))

            def row_maxima(b):
                row_max = stats.tile([T, TILES_PER_BANK], F32, name="row_max")
                nc.vector.tensor_reduce(
                    row_max[:],
                    scores_of[b][:].rearrange("t (i u) -> t i u", i=TILES_PER_BANK),
                    axis=mybir.AxisListType.X,
                    op=ALU.max,
                )
                shift = stats.tile([T, TILES_PER_BANK], F32, name="shift")
                nc.vector.tensor_scalar(shift[:], row_max[:], -SCALE, None, op0=ALU.mult)
                shift_of[b] = shift

            def exponentials(b):
                weights = work.tile([T, TILES_PER_BANK, T], BF16, name="weights")
                row_sum = stats.tile([T, TILES_PER_BANK], F32, name="row_sum")
                for i in range(TILES_PER_BANK):
                    nc.scalar.activation(
                        weights[:, i, :],
                        scores_of[b][:, i * T : (i + 1) * T],
                        ACT.Exp,
                        bias=shift_of[b][:, i : i + 1],
                        scale=SCALE,
                        accum_out=row_sum[:, i : i + 1],
                    )
                weights_of[b] = weights
                row_sum_of[b] = row_sum

            def flips(b):
                flip_ps = psum.tile([T, TILES_PER_BANK, T], BF16, name="flip_ps", tag="flip")
                for i in range(TILES_PER_BANK):
                    nc.tensor.transpose(flip_ps[:, i, :], weights_of[b][:, i, :], ident[:])
                flip_ps_of[b] = flip_ps

            def flip_copy(b):
                weights_flip = work.tile([T, TILES_PER_BANK, T], BF16, name="weights_flip")
                nc.scalar.copy(weights_flip[:], flip_ps_of[b][:])
                weights_flip_of[b] = weights_flip

            def value_matmuls(b):
                g, bank = divmod(b, BANKS_PER_LOAD)
                v_t = loaded[g][2]
                out_ps = psum.tile([T, TILES_PER_BANK, DH], F32, name="out_ps", tag="out")
                for i in range(TILES_PER_BANK):
                    nc.tensor.matmul(
                        out_ps[:, i, :],
                        weights_flip_of[b][:, i, :],
                        v_t[:, bank * TILES_PER_BANK + i, :],
                        start=True,
                        stop=True,
                    )
                out_ps_of[b] = out_ps
                if bank == BANKS_PER_LOAD - 1 and g + PREFETCH < FIRST_REUSE:
                    loaded.append(load_group(g + PREFETCH))

            def normalise(b):
                g, bank = divmod(b, BANKS_PER_LOAD)
                if bank == 0:
                    staged_of[g] = staging.tile([T, TILES_PER_LOAD, DH], F32, name="staged")
                inv_sum = stats.tile([T, TILES_PER_BANK], F32, name="inv_sum")
                nc.vector.reciprocal(inv_sum[:], row_sum_of[b][:])
                nc.vector.tensor_tensor(
                    staged_of[g][:, bank * TILES_PER_BANK : (bank + 1) * TILES_PER_BANK, :],
                    out_ps_of[b][:],
                    inv_sum[:].unsqueeze(2).to_broadcast([T, TILES_PER_BANK, DH]),
                    op=ALU.mult,
                )
                if g == N_LOADS - 1:
                    heads = slice(b * HEADS_PER_BANK, (b + 1) * HEADS_PER_BANK)
                    tiles = slice(bank * TILES_PER_BANK, (bank + 1) * TILES_PER_BANK)
                    nc.scalar.dma_start(out[heads].rearrange("h n t d -> t (h n) d"), staged_of[g][:, tiles, :])
                elif bank == BANKS_PER_LOAD - 1:
                    heads = slice(g * HEADS_PER_LOAD, (g + 1) * HEADS_PER_LOAD)
                    nc.scalar.dma_start(out[heads].rearrange("h n t d -> t (h n) d"), staged_of[g][:])

            def run(stage, b):
                if 0 <= b < N_BANKS:
                    stage(b)

            for s in range(N_BANKS + 6):
                run(score_matmuls, s)
                run(row_maxima, s - 1)
                run(exponentials, s - 2)
                run(flips, s - 3)
                run(flip_copy, s - 4)
                run(value_matmuls, s - 5)
                run(normalise, s - 6)
